import numpy as np
import ml_dtypes


def mxq(x, axis, fmt="e4m3"):
    dtype, down = {"e4m3": (ml_dtypes.float8_e4m3fn, 7), "e5m2": (ml_dtypes.float8_e5m2, 14)}[fmt]
    v = np.moveaxis(np.asarray(x, np.float32).astype(ml_dtypes.bfloat16).astype(np.float64), axis, -1)
    blocks = v.reshape(v.shape[:-1] + (-1, 32))
    amax = np.abs(blocks).max(-1, keepdims=True)
    byte = np.maximum(np.where(amax > 0, np.frexp(amax)[1] - 1 + 127, 0) - down, 1)
    scale = np.exp2(byte - 127.0)
    codes = (blocks / scale).astype(np.float32).astype(dtype).astype(np.float64)
    return np.moveaxis((codes * scale).reshape(v.shape), -1, axis)


WIDE = False


def mx_kscale(k):
    if not WIDE:
        return np.ones(k)
    levels = np.array([10, -10, 5, -5, 0])
    a = np.random.permutation(np.resize(levels, k // 512 * 4)).reshape(k // 512, 4)
    idx = np.arange(k)
    return np.exp2(a[idx // 512, idx % 128 // 32])


BF16 = ml_dtypes.bfloat16


def bf(x):
    return np.asarray(x, np.float32).astype(BF16)


def f64(x):
    return np.asarray(x).astype(np.float64)


B, S, HIDDEN, Q_LORA, NUM_HEADS, QK_NOPE, QK_ROPE, KV_LORA = 2, 64, 512, 512, 16, 128, 64, 64
QK_HEAD = QK_NOPE + QK_ROPE


def rotate_half(t):
    d = t.shape[-1] // 2
    return np.concatenate([-t[..., d:], t[..., :d]], axis=-1)


def setup_inputs():
    s, t = mx_kscale(HIDDEN), mx_kscale(Q_LORA)
    x = bf(np.random.standard_normal((B, S, HIDDEN)) * s)
    cos = bf(np.random.uniform(size=(B, S, QK_ROPE)))
    sin = bf(np.random.uniform(size=(B, S, QK_ROPE)))
    Wqa = bf(np.random.standard_normal((Q_LORA, HIDDEN)) / np.sqrt(HIDDEN) * t[:, None] / s)
    Wqb = bf(np.random.standard_normal((NUM_HEADS * QK_HEAD, Q_LORA)) / np.sqrt(Q_LORA) / t)
    Wkva = bf(np.random.standard_normal((KV_LORA + QK_ROPE, HIDDEN)) / np.sqrt(HIDDEN) / s)
    return {"x": x, "cos": cos, "sin": sin, "Wqa": Wqa, "Wqb": Wqb, "Wkva": Wkva}


def reference(x, cos, sin, Wqa, Wqb, Wkva):
    b, s, _ = x.shape
    xq = mxq(f64(x), 2, "e4m3")
    qa = xq @ mxq(f64(Wqa), 1, "e4m3").T
    q = (mxq(qa, 2, "e4m3") @ mxq(f64(Wqb), 1, "e4m3").T).reshape(b, s, NUM_HEADS, QK_HEAD)
    q_nope = q[..., :QK_NOPE]
    q_pe = q[..., QK_NOPE:]
    kv = xq @ mxq(f64(Wkva), 1, "e4m3").T
    compressed_kv = kv[..., :KV_LORA]
    k_pe = kv[..., KV_LORA:].reshape(b, s, 1, QK_ROPE)
    c = f64(cos)[:, :, None, :]
    sn = f64(sin)[:, :, None, :]
    q_pe_rot = q_pe * c + rotate_half(q_pe) * sn
    k_pe_rot = k_pe * c + rotate_half(k_pe) * sn
    q_out = np.concatenate([q_nope, q_pe_rot], axis=-1).reshape(b, s, -1)
    k_out = k_pe_rot.reshape(b, s, QK_ROPE)
    return np.concatenate([q_out, k_out, compressed_kv], axis=-1)

@@ -1,0 +1,198 @@
+from contextlib import ExitStack
+
+import concourse.masks as masks
+import concourse.mybir as mybir
+
+F32 = mybir.dt.float32
+BF16 = mybir.dt.bfloat16
+U32 = mybir.dt.uint32
+U8 = mybir.dt.uint8
+FP8X4 = mybir.dt.float8_e4m3fn_x4
+MULT = mybir.AluOpType.mult
+ADD = mybir.AluOpType.add
+
+P = 128
+K = 512
+PACK = 4
+WORDS = K // 2
+PLANES_PER_BANK = 4
+HEADS = 16
+UNIT = 64
+HALF = UNIT // 2
+UNITS_PER_HEAD = 3
+Q_COLS = HEADS * UNITS_PER_HEAD * UNIT
+CHUNK = 512
+CHUNKS = Q_COLS // CHUNK
+ROWS_PER_PARTITION = CHUNK // P
+UNITS_PER_CHUNK = CHUNK // UNIT
+LEAD = 2
+
+FLOPS = 2 * P * K * (K + Q_COLS + P)
+
+
+def transpose_four_planes(nc, planes_psum, raw, first_plane, identity):
+    words = raw[:].bitcast(F32)
+    bank = planes_psum.tile([P, PLANES_PER_BANK, P], F32, tag="planes")
+    for i in range(PLANES_PER_BANK):
+        plane = first_plane + i
+        nc.tensor.transpose(bank[:, i, :], words[:, plane * P : (plane + 1) * P], identity[:])
+    return bank
+
+
+def rotate(nc, stream, rotary, cos_sb, sin_sb, result, heads):
+    cos_all = cos_sb[:].unsqueeze(1).to_broadcast([P, heads, UNIT])
+    sin_low = sin_sb[:, 0:HALF].unsqueeze(1).to_broadcast([P, heads, HALF])
+    sin_high = sin_sb[:, HALF:UNIT].unsqueeze(1).to_broadcast([P, heads, HALF])
+    crossed = stream.tile([P, UNITS_PER_HEAD, UNIT], F32, tag="crossed")
+    nc.vector.tensor_tensor(out=result, in0=rotary, in1=cos_all, op=MULT)
+    nc.vector.tensor_tensor(
+        out=crossed[:, 0:heads, 0:HALF], in0=rotary[:, :, HALF:UNIT], in1=sin_low, op=MULT
+    )
+    nc.vector.tensor_tensor(
+        out=crossed[:, 0:heads, HALF:UNIT], in0=rotary[:, :, 0:HALF], in1=sin_high, op=MULT
+    )
+    nc.vector.tensor_tensor(out=result, in0=result, in1=crossed[:, 0:heads, :], op=ADD)
+
+
+def tile_mlaselfattn_s_kernel(tc, x, cos, sin, Wqa, Wqb, Wkva, out):
+    nc = tc.nc
+    out_rows = out.flatten_outer_dims()
+
+    with ExitStack() as ctx:
+        keep = ctx.enter_context(tc.tile_pool(name="keep", bufs=1))
+        stream = ctx.enter_context(tc.tile_pool(name="stream", bufs=3))
+        planes_psum = ctx.enter_context(tc.psum_pool(name="planes_psum", bufs=4))
+        sums_psum = ctx.enter_context(tc.psum_pool(name="sums_psum", bufs=4))
+
+        identity = keep.tile([P, P], F32)
+        masks.make_identity(nc, identity[:])
+
+        xk_raw = keep.tile([P, 2 * K], BF16)
+        nc.sync.dma_start(out=xk_raw[:, 0:K], in_=x.flatten_outer_dims())
+        nc.sync.dma_start(out=xk_raw[:, K : 2 * K], in_=Wkva)
+        wqa_raw = keep.tile([P, PACK * K], BF16)
+        nc.sync.dma_start(
+            out=wqa_raw[:].rearrange("p (u eh) -> p u eh", u=2),
+            in_=Wqa.rearrange("(u p e) h -> p u (e h)", u=2, e=2),
+        )
+        wqb_raw = []
+        for c in range(CHUNKS):
+            raw = keep.tile([P, ROWS_PER_PARTITION * K], BF16, name="wqb_raw%d" % c)
+            nc.sync.dma_start(
+                out=raw[:],
+                in_=Wqb[c * CHUNK : (c + 1) * CHUNK, :].rearrange(
+                    "(p j) k -> p (j k)", j=ROWS_PER_PARTITION
+                ),
+            )
+            wqb_raw.append(raw)
+        cos_sb = keep.tile([P, UNIT], BF16)
+        sin_sb = keep.tile([P, UNIT], BF16)
+        nc.scalar.dma_start(out=cos_sb[:], in_=cos.flatten_outer_dims())
+        nc.scalar.dma_start(out=sin_sb[:], in_=sin.flatten_outer_dims())
+        nc.vector.tensor_scalar_mul(out=sin_sb[:, 0:HALF], in0=sin_sb[:, 0:HALF], scalar1=-1.0)
+
+        xk_codes = keep.tile([P, 2 * P], U32, align_bytes=64)
+        xk_scales = keep.tile([P, 2 * P], U8, align_bytes=64)
+        wqa_codes = keep.tile([P, K], U32, align_bytes=64)
+        wqa_scales = keep.tile([P, K], U8, align_bytes=64)
+        qa_codes = keep.tile([P, P], U32, align_bytes=64)
+        qa_scales = keep.tile([P, P], U8, align_bytes=64)
+        wqb_codes = keep.tile([P, CHUNKS, CHUNK], U32, align_bytes=64)
+        wqb_scales = keep.tile([P, CHUNKS, CHUNK], U8, align_bytes=64)
+        out_sb = keep.tile([P, Q_COLS + 2 * UNIT], F32)
+
+        def prepare_blocks(raw, first_plane, codes, scales):
+            bank = transpose_four_planes(nc, planes_psum, raw, first_plane, identity)
+            grouped = stream.tile([P, 2 * P * PACK], BF16, tag="grouped_blocks", align_bytes=64)
+            nc.scalar.copy(
+                out=grouped[:].bitcast(F32).rearrange("k (r c u) -> k r c u", r=2, u=2),
+                in_=bank[:].rearrange("k (r u) c -> k r c u", u=2),
+            )
+            nc.vector.quantize_mx(out=codes.bitcast(FP8X4), scales=scales, in_=grouped[:])
+
+        def prepare_chunk(c):
+            grouped = stream.tile([P, CHUNK * PACK], BF16, tag="grouped_chunk", align_bytes=64)
+            grouped_words = grouped[:].bitcast(F32).rearrange(
+                "k (c m) -> k c m", m=2 * ROWS_PER_PARTITION
+            )
+            for b in range(2):
+                first_plane = b * PLANES_PER_BANK
+                bank = transpose_four_planes(nc, planes_psum, wqb_raw[c], first_plane, identity)
+                nc.scalar.copy(
+                    out=grouped_words[:, :, first_plane : first_plane + PLANES_PER_BANK],
+                    in_=bank[:].rearrange("k m c -> k c m"),
+                )
+            nc.vector.quantize_mx(
+                out=wqb_codes[:, c, :].bitcast(FP8X4), scales=wqb_scales[:, c, :], in_=grouped[:]
+            )
+
+        def finish_chunk(c):
+            q_ps = sums_psum.tile([P, CHUNK], F32, tag="sums")
+            nc.tensor.matmul_mx(
+                out=q_ps[:],
+                lhsT=qa_codes[:].bitcast(FP8X4),
+                lhsT_scale=qa_scales[:],
+                rhs=wqb_codes[:, c, :].bitcast(FP8X4),
+                rhs_scale=wqb_scales[:, c, :],
+                start=True,
+                stop=True,
+            )
+            q_units = q_ps[:].rearrange("p (g w) -> p g w", w=UNIT)
+            out_units = out_sb[:, c * CHUNK : (c + 1) * CHUNK].rearrange("p (g w) -> p g w", w=UNIT)
+            for part in range(UNITS_PER_HEAD):
+                first = (part - c * UNITS_PER_CHUNK) % UNITS_PER_HEAD
+                source = q_units[:, first::UNITS_PER_HEAD, :]
+                target = out_units[:, first::UNITS_PER_HEAD, :]
+                if part < UNITS_PER_HEAD - 1:
+                    nc.scalar.copy(out=target, in_=source)
+                else:
+                    rotate(nc, stream, source, cos_sb, sin_sb, target, source.shape[1])
+
+        prepare_blocks(xk_raw, 0, xk_codes[:], xk_scales[:])
+        for b in range(2):
+            cols = slice(b * 2 * P, (b + 1) * 2 * P)
+            prepare_blocks(wqa_raw, b * PLANES_PER_BANK, wqa_codes[:, cols], wqa_scales[:, cols])
+        prepare_chunk(0)
+
+        qaT_ps = sums_psum.tile([P, PACK, P], F32, tag="sums")
+        for t in range(PACK):
+            nc.tensor.matmul_mx(
+                out=qaT_ps[:, t, :],
+                lhsT=wqa_codes[:, t * P : (t + 1) * P].bitcast(FP8X4),
+                lhsT_scale=wqa_scales[:, t * P : (t + 1) * P],
+                rhs=xk_codes[:, 0:P].bitcast(FP8X4),
+                rhs_scale=xk_scales[:, 0:P],
+                start=True,
+                stop=True,
+            )
+        qa_grouped = keep.tile([P, P, PACK], BF16, align_bytes=64)
+        nc.vector.tensor_copy(out=qa_grouped[:], in_=qaT_ps[:].rearrange("k t n -> k n t"))
+        prepare_chunk(1)
+        nc.vector.quantize_mx(
+            out=qa_codes[:].bitcast(FP8X4),
+            scales=qa_scales[:],
+            in_=qa_grouped[:].rearrange("k n t -> k (n t)"),
+        )
+
+        kv_ps = sums_psum.tile([P, 2, UNIT], F32, tag="sums")
+        nc.tensor.matmul_mx(
+            out=kv_ps[:].rearrange("p g w -> p (g w)"),
+            lhsT=xk_codes[:, 0:P].bitcast(FP8X4),
+            lhsT_scale=xk_scales[:, 0:P],
+            rhs=xk_codes[:, P : 2 * P].bitcast(FP8X4),
+            rhs_scale=xk_scales[:, P : 2 * P],
+            start=True,
+            stop=True,
+        )
+        tail_units = out_sb[:, Q_COLS : Q_COLS + 2 * UNIT].rearrange("p (g w) -> p g w", w=UNIT)
+        nc.scalar.copy(out=tail_units[:, 1:2, :], in_=kv_ps[:, 0:1, :])
+        rotate(nc, stream, kv_ps[:, 1:2, :], cos_sb, sin_sb, tail_units[:, 0:1, :], 1)
+
+        for c in range(CHUNKS):
+            if c + LEAD < CHUNKS:
+                prepare_chunk(c + LEAD)
+            finish_chunk(c)
+            last = c * CHUNK + CHUNK if c < CHUNKS - 1 else Q_COLS + 2 * UNIT
+            nc.sync.dma_start(
+                out=out_rows[:, c * CHUNK : last], in_=out_sb[:, c * CHUNK : last]
+            )

@@ -5,6 +5,7 @@ import concourse.mybir as mybir
 
 F32 = mybir.dt.float32
 BF16 = mybir.dt.bfloat16
+I32 = mybir.dt.int32
 U32 = mybir.dt.uint32
 U8 = mybir.dt.uint8
 FP8X4 = mybir.dt.float8_e4m3fn_x4
@@ -14,7 +15,6 @@ ADD = mybir.AluOpType.add
 P = 128
 K = 512
 PACK = 4
-WORDS = K // 2
 PLANES_PER_BANK = 4
 HEADS = 16
 UNIT = 64
@@ -26,20 +26,21 @@ CHUNKS = Q_COLS // CHUNK
 ROWS_PER_PARTITION = CHUNK // P
 UNITS_PER_CHUNK = CHUNK // UNIT
 LEAD = 2
+WARM_PASSES = 4
 
 FLOPS = 2 * P * K * (K + Q_COLS + P)
 
 
-def transpose_four_planes(nc, planes_psum, raw, first_plane, identity):
+def transpose_planes(nc, planes_psum, raw, first_plane, planes, identity):
     words = raw[:].bitcast(F32)
-    bank = planes_psum.tile([P, PLANES_PER_BANK, P], F32, tag="planes")
-    for i in range(PLANES_PER_BANK):
+    bank = planes_psum.tile([P, planes, P], F32, tag="planes")
+    for i in range(planes):
         plane = first_plane + i
         nc.tensor.transpose(bank[:, i, :], words[:, plane * P : (plane + 1) * P], identity[:])
     return bank
 
 
-def rotate(nc, stream, rotary, cos_sb, sin_sb, result, heads):
+def rotary_products(nc, stream, rotary, cos_sb, sin_sb, result, heads):
     cos_all = cos_sb[:].unsqueeze(1).to_broadcast([P, heads, UNIT])
     sin_low = sin_sb[:, 0:HALF].unsqueeze(1).to_broadcast([P, heads, HALF])
     sin_high = sin_sb[:, HALF:UNIT].unsqueeze(1).to_broadcast([P, heads, HALF])
@@ -51,7 +52,7 @@ def rotate(nc, stream, rotary, cos_sb, sin_sb, result, heads):
     nc.vector.tensor_tensor(
         out=crossed[:, 0:heads, HALF:UNIT], in0=rotary[:, :, 0:HALF], in1=sin_high, op=MULT
     )
-    nc.vector.tensor_tensor(out=result, in0=result, in1=crossed[:, 0:heads, :], op=ADD)
+    return crossed[:, 0:heads, :]
 
 
 def tile_mlaselfattn_s_kernel(tc, x, cos, sin, Wqa, Wqb, Wkva, out):
@@ -62,19 +63,43 @@ def tile_mlaselfattn_s_kernel(tc, x, cos, sin, Wqa, Wqb, Wkva, out):
         keep = ctx.enter_context(tc.tile_pool(name="keep", bufs=1))
         stream = ctx.enter_context(tc.tile_pool(name="stream", bufs=3))
         planes_psum = ctx.enter_context(tc.psum_pool(name="planes_psum", bufs=4))
-        sums_psum = ctx.enter_context(tc.psum_pool(name="sums_psum", bufs=4))
+        sums_psum = ctx.enter_context(tc.psum_pool(name="sums_psum", bufs=3))
+        spare_psum = ctx.enter_context(tc.psum_pool(name="spare_psum", bufs=1))
+        ctx.enter_context(tc.manual_schedule())
+
+        zeros = keep.tile([P, CHUNK * PACK], BF16, align_bytes=64)
+        spare_codes = keep.tile([P, CHUNK], U32, align_bytes=64)
+        spare_scales = keep.tile([P, CHUNK], U8, align_bytes=64)
+        nc.vector.memset(zeros[:].bitcast(I32), 0)
+        nc.vector.quantize_mx(out=spare_codes[:].bitcast(FP8X4), scales=spare_scales[:], in_=zeros[:])
+        spare_ps = spare_psum.tile([P, CHUNK], F32)
+
+        def spare_pass():
+            nc.tensor.matmul_mx(
+                out=spare_ps[:],
+                lhsT=spare_codes[:, 0:P].bitcast(FP8X4),
+                lhsT_scale=spare_scales[:, 0:P],
+                rhs=spare_codes[:].bitcast(FP8X4),
+                rhs_scale=spare_scales[:],
+                start=True,
+                stop=True,
+            )
 
         identity = keep.tile([P, P], F32)
         masks.make_identity(nc, identity[:])
 
-        xk_raw = keep.tile([P, 2 * K], BF16)
-        nc.sync.dma_start(out=xk_raw[:, 0:K], in_=x.flatten_outer_dims())
-        nc.sync.dma_start(out=xk_raw[:, K : 2 * K], in_=Wkva)
-        wqa_raw = keep.tile([P, PACK * K], BF16)
-        nc.sync.dma_start(
-            out=wqa_raw[:].rearrange("p (u eh) -> p u eh", u=2),
-            in_=Wqa.rearrange("(u p e) h -> p u (e h)", u=2, e=2),
-        )
+        x_raw = keep.tile([P, K], BF16)
+        nc.sync.dma_start(out=x_raw[:], in_=x.flatten_outer_dims())
+        wqa_raw = []
+        for u in range(2):
+            raw = keep.tile([P, 2 * K], BF16, name="wqa_raw%d" % u)
+            nc.sync.dma_start(
+                out=raw[:],
+                in_=Wqa[u * 2 * P : (u + 1) * 2 * P, :].rearrange("(p e) h -> p (e h)", e=2),
+            )
+            wqa_raw.append(raw)
+        kva_raw = keep.tile([P, K], BF16)
+        nc.sync.dma_start(out=kva_raw[:], in_=Wkva)
         wqb_raw = []
         for c in range(CHUNKS):
             raw = keep.tile([P, ROWS_PER_PARTITION * K], BF16, name="wqb_raw%d" % c)
@@ -89,10 +114,11 @@ def tile_mlaselfattn_s_kernel(tc, x, cos, sin, Wqa, Wqb, Wkva, out):
         sin_sb = keep.tile([P, UNIT], BF16)
         nc.scalar.dma_start(out=cos_sb[:], in_=cos.flatten_outer_dims())
         nc.scalar.dma_start(out=sin_sb[:], in_=sin.flatten_outer_dims())
-        nc.vector.tensor_scalar_mul(out=sin_sb[:, 0:HALF], in0=sin_sb[:, 0:HALF], scalar1=-1.0)
 
-        xk_codes = keep.tile([P, 2 * P], U32, align_bytes=64)
-        xk_scales = keep.tile([P, 2 * P], U8, align_bytes=64)
+        x_codes = keep.tile([P, P], U32, align_bytes=64)
+        x_scales = keep.tile([P, P], U8, align_bytes=64)
+        kva_codes = keep.tile([P, P], U32, align_bytes=64)
+        kva_scales = keep.tile([P, P], U8, align_bytes=64)
         wqa_codes = keep.tile([P, K], U32, align_bytes=64)
         wqa_scales = keep.tile([P, K], U8, align_bytes=64)
         qa_codes = keep.tile([P, P], U32, align_bytes=64)
@@ -101,32 +127,42 @@ def tile_mlaselfattn_s_kernel(tc, x, cos, sin, Wqa, Wqb, Wkva, out):
         wqb_scales = keep.tile([P, CHUNKS, CHUNK], U8, align_bytes=64)
         out_sb = keep.tile([P, Q_COLS + 2 * UNIT], F32)
 
-        def prepare_blocks(raw, first_plane, codes, scales):
-            bank = transpose_four_planes(nc, planes_psum, raw, first_plane, identity)
-            grouped = stream.tile([P, 2 * P * PACK], BF16, tag="grouped_blocks", align_bytes=64)
+        def prepare_blocks(raw, slots, codes, scales):
+            bank = transpose_planes(nc, planes_psum, raw, 0, 2 * slots, identity)
+            grouped = stream.tile([P, slots * P * PACK], BF16, tag="grouped_blocks", align_bytes=64)
             nc.scalar.copy(
-                out=grouped[:].bitcast(F32).rearrange("k (r c u) -> k r c u", r=2, u=2),
+                out=grouped[:].bitcast(F32).rearrange("k (r c u) -> k r c u", r=slots, u=2),
                 in_=bank[:].rearrange("k (r u) c -> k r c u", u=2),
             )
             nc.vector.quantize_mx(out=codes.bitcast(FP8X4), scales=scales, in_=grouped[:])
 
-        def prepare_chunk(c):
-            grouped = stream.tile([P, CHUNK * PACK], BF16, tag="grouped_chunk", align_bytes=64)
+        grouped_chunks = {}
+
+        def transpose_chunk(c):
+            grouped = stream.tile(
+                [P, CHUNK * PACK], BF16, tag="grouped_chunk", name="grouped%d" % c, align_bytes=64
+            )
             grouped_words = grouped[:].bitcast(F32).rearrange(
                 "k (c m) -> k c m", m=2 * ROWS_PER_PARTITION
             )
-            for b in range(2):
-                first_plane = b * PLANES_PER_BANK
-                bank = transpose_four_planes(nc, planes_psum, wqb_raw[c], first_plane, identity)
+            for first in range(0, 2 * ROWS_PER_PARTITION, PLANES_PER_BANK):
+                bank = transpose_planes(
+                    nc, planes_psum, wqb_raw[c], first, PLANES_PER_BANK, identity
+                )
                 nc.scalar.copy(
-                    out=grouped_words[:, :, first_plane : first_plane + PLANES_PER_BANK],
+                    out=grouped_words[:, :, first : first + PLANES_PER_BANK],
                     in_=bank[:].rearrange("k m c -> k c m"),
                 )
+            grouped_chunks[c] = grouped
+
+        def quantise_chunk(c):
             nc.vector.quantize_mx(
-                out=wqb_codes[:, c, :].bitcast(FP8X4), scales=wqb_scales[:, c, :], in_=grouped[:]
+                out=wqb_codes[:, c, :].bitcast(FP8X4),
+                scales=wqb_scales[:, c, :],
+                in_=grouped_chunks[c][:],
             )
 
-        def finish_chunk(c):
+        def multiply_chunk(c):
             q_ps = sums_psum.tile([P, CHUNK], F32, tag="sums")
             nc.tensor.matmul_mx(
                 out=q_ps[:],
@@ -137,22 +173,34 @@ def tile_mlaselfattn_s_kernel(tc, x, cos, sin, Wqa, Wqb, Wkva, out):
                 start=True,
                 stop=True,
             )
+            return q_ps
+
+        def finish_chunk(c, q_ps):
             q_units = q_ps[:].rearrange("p (g w) -> p g w", w=UNIT)
             out_units = out_sb[:, c * CHUNK : (c + 1) * CHUNK].rearrange("p (g w) -> p g w", w=UNIT)
+            source = []
+            target = []
             for part in range(UNITS_PER_HEAD):
                 first = (part - c * UNITS_PER_CHUNK) % UNITS_PER_HEAD
-                source = q_units[:, first::UNITS_PER_HEAD, :]
-                target = out_units[:, first::UNITS_PER_HEAD, :]
-                if part < UNITS_PER_HEAD - 1:
-                    nc.scalar.copy(out=target, in_=source)
-                else:
-                    rotate(nc, stream, source, cos_sb, sin_sb, target, source.shape[1])
+                source.append(q_units[:, first::UNITS_PER_HEAD, :])
+                target.append(out_units[:, first::UNITS_PER_HEAD, :])
+            nc.scalar.copy(out=target[0], in_=source[0])
+            crossed = rotary_products(
+                nc, stream, source[2], cos_sb, sin_sb, target[2], source[2].shape[1]
+            )
+            nc.vector.tensor_copy(out=target[1], in_=source[1])
+            nc.vector.tensor_tensor(out=target[2], in0=target[2], in1=crossed, op=ADD)
+            last = (c + 1) * CHUNK if c < CHUNKS - 1 else Q_COLS + 2 * UNIT
+            nc.sync.dma_start(out=out_rows[:, c * CHUNK : last], in_=out_sb[:, c * CHUNK : last])
 
-        prepare_blocks(xk_raw, 0, xk_codes[:], xk_scales[:])
-        for b in range(2):
-            cols = slice(b * 2 * P, (b + 1) * 2 * P)
-            prepare_blocks(wqa_raw, b * PLANES_PER_BANK, wqa_codes[:, cols], wqa_scales[:, cols])
-        prepare_chunk(0)
+        for i in range(WARM_PASSES):
+            spare_pass()
+        prepare_blocks(x_raw, 1, x_codes[:], x_scales[:])
+        for u in range(2):
+            cols = slice(u * 2 * P, (u + 1) * 2 * P)
+            spare_pass()
+            prepare_blocks(wqa_raw[u], 2, wqa_codes[:, cols], wqa_scales[:, cols])
+        prepare_blocks(kva_raw, 1, kva_codes[:], kva_scales[:])
 
         qaT_ps = sums_psum.tile([P, PACK, P], F32, tag="sums")
         for t in range(PACK):
@@ -160,14 +208,16 @@ def tile_mlaselfattn_s_kernel(tc, x, cos, sin, Wqa, Wqb, Wkva, out):
                 out=qaT_ps[:, t, :],
                 lhsT=wqa_codes[:, t * P : (t + 1) * P].bitcast(FP8X4),
                 lhsT_scale=wqa_scales[:, t * P : (t + 1) * P],
-                rhs=xk_codes[:, 0:P].bitcast(FP8X4),
-                rhs_scale=xk_scales[:, 0:P],
+                rhs=x_codes[:].bitcast(FP8X4),
+                rhs_scale=x_scales[:],
                 start=True,
                 stop=True,
             )
         qa_grouped = keep.tile([P, P, PACK], BF16, align_bytes=64)
         nc.vector.tensor_copy(out=qa_grouped[:], in_=qaT_ps[:].rearrange("k t n -> k n t"))
-        prepare_chunk(1)
+        spare_pass()
+        transpose_chunk(0)
+        quantise_chunk(0)
         nc.vector.quantize_mx(
             out=qa_codes[:].bitcast(FP8X4),
             scales=qa_scales[:],
@@ -177,22 +227,29 @@ def tile_mlaselfattn_s_kernel(tc, x, cos, sin, Wqa, Wqb, Wkva, out):
         kv_ps = sums_psum.tile([P, 2, UNIT], F32, tag="sums")
         nc.tensor.matmul_mx(
             out=kv_ps[:].rearrange("p g w -> p (g w)"),
-            lhsT=xk_codes[:, 0:P].bitcast(FP8X4),
-            lhsT_scale=xk_scales[:, 0:P],
-            rhs=xk_codes[:, P : 2 * P].bitcast(FP8X4),
-            rhs_scale=xk_scales[:, P : 2 * P],
+            lhsT=x_codes[:].bitcast(FP8X4),
+            lhsT_scale=x_scales[:],
+            rhs=kva_codes[:].bitcast(FP8X4),
+            rhs_scale=kva_scales[:],
             start=True,
             stop=True,
         )
+        spare_pass()
+        transpose_chunk(1)
         tail_units = out_sb[:, Q_COLS : Q_COLS + 2 * UNIT].rearrange("p (g w) -> p g w", w=UNIT)
         nc.scalar.copy(out=tail_units[:, 1:2, :], in_=kv_ps[:, 0:1, :])
-        rotate(nc, stream, kv_ps[:, 1:2, :], cos_sb, sin_sb, tail_units[:, 0:1, :], 1)
+        nc.vector.tensor_scalar_mul(out=sin_sb[:, 0:HALF], in0=sin_sb[:, 0:HALF], scalar1=-1.0)
+        crossed = rotary_products(
+            nc, stream, kv_ps[:, 1:2, :], cos_sb, sin_sb, tail_units[:, 0:1, :], 1
+        )
+        nc.vector.tensor_tensor(
+            out=tail_units[:, 0:1, :], in0=tail_units[:, 0:1, :], in1=crossed, op=ADD
+        )
 
         for c in range(CHUNKS):
             if c + LEAD < CHUNKS:
-                prepare_chunk(c + LEAD)
-            finish_chunk(c)
-            last = c * CHUNK + CHUNK if c < CHUNKS - 1 else Q_COLS + 2 * UNIT
-            nc.sync.dma_start(
-                out=out_rows[:, c * CHUNK : last], in_=out_sb[:, c * CHUNK : last]
-            )
+                transpose_chunk(c + LEAD)
+            q_ps = multiply_chunk(c)
+            if c + 1 < CHUNKS:
+                quantise_chunk(c + 1)
+            finish_chunk(c, q_ps)

@@ -5,7 +5,6 @@ import concourse.mybir as mybir
 
 F32 = mybir.dt.float32
 BF16 = mybir.dt.bfloat16
-I32 = mybir.dt.int32
 U32 = mybir.dt.uint32
 U8 = mybir.dt.uint8
 FP8X4 = mybir.dt.float8_e4m3fn_x4
@@ -22,11 +21,11 @@ HALF = UNIT // 2
 UNITS_PER_HEAD = 3
 Q_COLS = HEADS * UNITS_PER_HEAD * UNIT
 CHUNK = 512
-CHUNKS = Q_COLS // CHUNK
-ROWS_PER_PARTITION = CHUNK // P
-UNITS_PER_CHUNK = CHUNK // UNIT
+CHUNK_ROWS = [CHUNK] * (Q_COLS // CHUNK - 1) + [CHUNK // 2, CHUNK // 2]
+CHUNKS = len(CHUNK_ROWS)
+CHUNK_START = [sum(CHUNK_ROWS[:c]) for c in range(CHUNKS)]
 LEAD = 2
-WARM_PASSES = 4
+LAG = 1
 
 FLOPS = 2 * P * K * (K + Q_COLS + P)
 
@@ -63,27 +62,8 @@ def tile_mlaselfattn_s_kernel(tc, x, cos, sin, Wqa, Wqb, Wkva, out):
         keep = ctx.enter_context(tc.tile_pool(name="keep", bufs=1))
         stream = ctx.enter_context(tc.tile_pool(name="stream", bufs=3))
         planes_psum = ctx.enter_context(tc.psum_pool(name="planes_psum", bufs=4))
-        sums_psum = ctx.enter_context(tc.psum_pool(name="sums_psum", bufs=3))
-        spare_psum = ctx.enter_context(tc.psum_pool(name="spare_psum", bufs=1))
+        sums_psum = ctx.enter_context(tc.psum_pool(name="sums_psum", bufs=4))
         ctx.enter_context(tc.manual_schedule())
-
-        zeros = keep.tile([P, CHUNK * PACK], BF16, align_bytes=64)
-        spare_codes = keep.tile([P, CHUNK], U32, align_bytes=64)
-        spare_scales = keep.tile([P, CHUNK], U8, align_bytes=64)
-        nc.vector.memset(zeros[:].bitcast(I32), 0)
-        nc.vector.quantize_mx(out=spare_codes[:].bitcast(FP8X4), scales=spare_scales[:], in_=zeros[:])
-        spare_ps = spare_psum.tile([P, CHUNK], F32)
-
-        def spare_pass():
-            nc.tensor.matmul_mx(
-                out=spare_ps[:],
-                lhsT=spare_codes[:, 0:P].bitcast(FP8X4),
-                lhsT_scale=spare_scales[:, 0:P],
-                rhs=spare_codes[:].bitcast(FP8X4),
-                rhs_scale=spare_scales[:],
-                start=True,
-                stop=True,
-            )
 
         identity = keep.tile([P, P], F32)
         masks.make_identity(nc, identity[:])
@@ -102,11 +82,11 @@ def tile_mlaselfattn_s_kernel(tc, x, cos, sin, Wqa, Wqb, Wkva, out):
         nc.sync.dma_start(out=kva_raw[:], in_=Wkva)
         wqb_raw = []
         for c in range(CHUNKS):
-            raw = keep.tile([P, ROWS_PER_PARTITION * K], BF16, name="wqb_raw%d" % c)
+            raw = keep.tile([P, CHUNK_ROWS[c] // P * K], BF16, name="wqb_raw%d" % c)
             nc.sync.dma_start(
                 out=raw[:],
-                in_=Wqb[c * CHUNK : (c + 1) * CHUNK, :].rearrange(
-                    "(p j) k -> p (j k)", j=ROWS_PER_PARTITION
+                in_=Wqb[CHUNK_START[c] : CHUNK_START[c] + CHUNK_ROWS[c], :].rearrange(
+                    "(p j) k -> p (j k)", p=P
                 ),
             )
             wqb_raw.append(raw)
@@ -123,8 +103,8 @@ def tile_mlaselfattn_s_kernel(tc, x, cos, sin, Wqa, Wqb, Wkva, out):
         wqa_scales = keep.tile([P, K], U8, align_bytes=64)
         qa_codes = keep.tile([P, P], U32, align_bytes=64)
         qa_scales = keep.tile([P, P], U8, align_bytes=64)
-        wqb_codes = keep.tile([P, CHUNKS, CHUNK], U32, align_bytes=64)
-        wqb_scales = keep.tile([P, CHUNKS, CHUNK], U8, align_bytes=64)
+        wqb_codes = keep.tile([P, Q_COLS], U32, align_bytes=64)
+        wqb_scales = keep.tile([P, Q_COLS], U8, align_bytes=64)
         out_sb = keep.tile([P, Q_COLS + 2 * UNIT], F32)
 
         def prepare_blocks(raw, slots, codes, scales):
@@ -139,68 +119,66 @@ def tile_mlaselfattn_s_kernel(tc, x, cos, sin, Wqa, Wqb, Wkva, out):
         grouped_chunks = {}
 
         def transpose_chunk(c):
+            planes = 2 * CHUNK_ROWS[c] // P
             grouped = stream.tile(
-                [P, CHUNK * PACK], BF16, tag="grouped_chunk", name="grouped%d" % c, align_bytes=64
+                [P, CHUNK_ROWS[c] * PACK], BF16, tag="grouped_chunk", name="grouped%d" % c,
+                align_bytes=64,
             )
-            grouped_words = grouped[:].bitcast(F32).rearrange(
-                "k (c m) -> k c m", m=2 * ROWS_PER_PARTITION
-            )
-            for first in range(0, 2 * ROWS_PER_PARTITION, PLANES_PER_BANK):
-                bank = transpose_planes(
-                    nc, planes_psum, wqb_raw[c], first, PLANES_PER_BANK, identity
-                )
+            grouped_words = grouped[:].bitcast(F32).rearrange("k (c m) -> k c m", m=planes)
+            for first in range(0, planes, PLANES_PER_BANK):
+                count = min(PLANES_PER_BANK, planes - first)
+                bank = transpose_planes(nc, planes_psum, wqb_raw[c], first, count, identity)
                 nc.scalar.copy(
-                    out=grouped_words[:, :, first : first + PLANES_PER_BANK],
+                    out=grouped_words[:, :, first : first + count],
                     in_=bank[:].rearrange("k m c -> k c m"),
                 )
             grouped_chunks[c] = grouped
 
+        def chunk_cols(c):
+            return slice(CHUNK_START[c], CHUNK_START[c] + CHUNK_ROWS[c])
+
         def quantise_chunk(c):
             nc.vector.quantize_mx(
-                out=wqb_codes[:, c, :].bitcast(FP8X4),
-                scales=wqb_scales[:, c, :],
+                out=wqb_codes[:, chunk_cols(c)].bitcast(FP8X4),
+                scales=wqb_scales[:, chunk_cols(c)],
                 in_=grouped_chunks[c][:],
             )
 
         def multiply_chunk(c):
-            q_ps = sums_psum.tile([P, CHUNK], F32, tag="sums")
+            q_ps = sums_psum.tile([P, CHUNK_ROWS[c]], F32, tag="sums")
             nc.tensor.matmul_mx(
                 out=q_ps[:],
                 lhsT=qa_codes[:].bitcast(FP8X4),
                 lhsT_scale=qa_scales[:],
-                rhs=wqb_codes[:, c, :].bitcast(FP8X4),
-                rhs_scale=wqb_scales[:, c, :],
+                rhs=wqb_codes[:, chunk_cols(c)].bitcast(FP8X4),
+                rhs_scale=wqb_scales[:, chunk_cols(c)],
                 start=True,
                 stop=True,
             )
             return q_ps
 
-        def finish_chunk(c, q_ps):
+        def chunk_parts(c, q_ps):
             q_units = q_ps[:].rearrange("p (g w) -> p g w", w=UNIT)
-            out_units = out_sb[:, c * CHUNK : (c + 1) * CHUNK].rearrange("p (g w) -> p g w", w=UNIT)
-            source = []
-            target = []
-            for part in range(UNITS_PER_HEAD):
-                first = (part - c * UNITS_PER_CHUNK) % UNITS_PER_HEAD
-                source.append(q_units[:, first::UNITS_PER_HEAD, :])
-                target.append(out_units[:, first::UNITS_PER_HEAD, :])
-            nc.scalar.copy(out=target[0], in_=source[0])
-            crossed = rotary_products(
-                nc, stream, source[2], cos_sb, sin_sb, target[2], source[2].shape[1]
-            )
-            nc.vector.tensor_copy(out=target[1], in_=source[1])
-            nc.vector.tensor_tensor(out=target[2], in0=target[2], in1=crossed, op=ADD)
-            last = (c + 1) * CHUNK if c < CHUNKS - 1 else Q_COLS + 2 * UNIT
-            nc.sync.dma_start(out=out_rows[:, c * CHUNK : last], in_=out_sb[:, c * CHUNK : last])
+            out_units = out_sb[:, chunk_cols(c)].rearrange("p (g w) -> p g w", w=UNIT)
+            first = [(part - CHUNK_START[c] // UNIT) % UNITS_PER_HEAD for part in range(UNITS_PER_HEAD)]
+            return [
+                (q_units[:, f::UNITS_PER_HEAD, :], out_units[:, f::UNITS_PER_HEAD, :]) for f in first
+            ]
 
-        for i in range(WARM_PASSES):
-            spare_pass()
+        def multiply_rotary(rotary, rotated):
+            crossed = rotary_products(nc, stream, rotary, cos_sb, sin_sb, rotated, rotary.shape[1])
+            return rotated, crossed
+
+        def add_rotary(products):
+            rotated, crossed = products
+            nc.vector.tensor_tensor(out=rotated, in0=rotated, in1=crossed, op=ADD)
+
         prepare_blocks(x_raw, 1, x_codes[:], x_scales[:])
         for u in range(2):
             cols = slice(u * 2 * P, (u + 1) * 2 * P)
-            spare_pass()
             prepare_blocks(wqa_raw[u], 2, wqa_codes[:, cols], wqa_scales[:, cols])
         prepare_blocks(kva_raw, 1, kva_codes[:], kva_scales[:])
+        transpose_chunk(0)
 
         qaT_ps = sums_psum.tile([P, PACK, P], F32, tag="sums")
         for t in range(PACK):
@@ -213,17 +191,6 @@ def tile_mlaselfattn_s_kernel(tc, x, cos, sin, Wqa, Wqb, Wkva, out):
                 start=True,
                 stop=True,
             )
-        qa_grouped = keep.tile([P, P, PACK], BF16, align_bytes=64)
-        nc.vector.tensor_copy(out=qa_grouped[:], in_=qaT_ps[:].rearrange("k t n -> k n t"))
-        spare_pass()
-        transpose_chunk(0)
-        quantise_chunk(0)
-        nc.vector.quantize_mx(
-            out=qa_codes[:].bitcast(FP8X4),
-            scales=qa_scales[:],
-            in_=qa_grouped[:].rearrange("k n t -> k (n t)"),
-        )
-
         kv_ps = sums_psum.tile([P, 2, UNIT], F32, tag="sums")
         nc.tensor.matmul_mx(
             out=kv_ps[:].rearrange("p g w -> p (g w)"),
@@ -234,22 +201,38 @@ def tile_mlaselfattn_s_kernel(tc, x, cos, sin, Wqa, Wqb, Wkva, out):
             start=True,
             stop=True,
         )
-        spare_pass()
+        qa_grouped = keep.tile([P, P, PACK], BF16, align_bytes=64)
+        nc.vector.tensor_copy(out=qa_grouped[:], in_=qaT_ps[:].rearrange("k t n -> k n t"))
+        quantise_chunk(0)
+        nc.vector.quantize_mx(
+            out=qa_codes[:].bitcast(FP8X4),
+            scales=qa_scales[:],
+            in_=qa_grouped[:].rearrange("k n t -> k (n t)"),
+        )
         transpose_chunk(1)
         tail_units = out_sb[:, Q_COLS : Q_COLS + 2 * UNIT].rearrange("p (g w) -> p g w", w=UNIT)
         nc.scalar.copy(out=tail_units[:, 1:2, :], in_=kv_ps[:, 0:1, :])
         nc.vector.tensor_scalar_mul(out=sin_sb[:, 0:HALF], in0=sin_sb[:, 0:HALF], scalar1=-1.0)
-        crossed = rotary_products(
-            nc, stream, kv_ps[:, 1:2, :], cos_sb, sin_sb, tail_units[:, 0:1, :], 1
-        )
-        nc.vector.tensor_tensor(
-            out=tail_units[:, 0:1, :], in0=tail_units[:, 0:1, :], in1=crossed, op=ADD
-        )
+        products = {-LAG: multiply_rotary(kv_ps[:, 1:2, :], tail_units[:, 0:1, :])}
 
-        for c in range(CHUNKS):
-            if c + LEAD < CHUNKS:
-                transpose_chunk(c + LEAD)
-            q_ps = multiply_chunk(c)
-            if c + 1 < CHUNKS:
-                quantise_chunk(c + 1)
-            finish_chunk(c, q_ps)
+        parts = {}
+        for step in range(CHUNKS + LAG):
+            ahead = step + LEAD
+            done = step - LAG
+            if ahead < CHUNKS:
+                transpose_chunk(ahead)
+            if step < CHUNKS:
+                parts[step] = chunk_parts(step, multiply_chunk(step))
+            if step + 1 < CHUNKS:
+                quantise_chunk(step + 1)
+            add_rotary(products[done])
+            if step < CHUNKS:
+                products[step] = multiply_rotary(parts[step][2][0], parts[step][2][1])
+            if done >= 0:
+                for part in range(UNITS_PER_HEAD - 1):
+                    nc.scalar.copy(out=parts[done][part][1], in_=parts[done][part][0])
+                first_col = CHUNK_START[done]
+                last_col = CHUNK_START[done + 1] if done + 1 < CHUNKS else Q_COLS + 2 * UNIT
+                nc.sync.dma_start(
+                    out=out_rows[:, first_col:last_col], in_=out_sb[:, first_col:last_col]
+                )

@@ -63,7 +63,6 @@ def tile_mlaselfattn_s_kernel(tc, x, cos, sin, Wqa, Wqb, Wkva, out):
         stream = ctx.enter_context(tc.tile_pool(name="stream", bufs=3))
         planes_psum = ctx.enter_context(tc.psum_pool(name="planes_psum", bufs=4))
         sums_psum = ctx.enter_context(tc.psum_pool(name="sums_psum", bufs=4))
-        ctx.enter_context(tc.manual_schedule())
 
         identity = keep.tile([P, P], F32)
         masks.make_identity(nc, identity[:])

@@ -21,7 +21,7 @@ HALF = UNIT // 2
 UNITS_PER_HEAD = 3
 Q_COLS = HEADS * UNITS_PER_HEAD * UNIT
 CHUNK = 512
-CHUNK_ROWS = [CHUNK] * (Q_COLS // CHUNK - 1) + [CHUNK // 2, CHUNK // 2]
+CHUNK_ROWS = [CHUNK] * (Q_COLS // CHUNK)
 CHUNKS = len(CHUNK_ROWS)
 CHUNK_START = [sum(CHUNK_ROWS[:c]) for c in range(CHUNKS)]
 LEAD = 2
@@ -63,6 +63,7 @@ def tile_mlaselfattn_s_kernel(tc, x, cos, sin, Wqa, Wqb, Wkva, out):
         stream = ctx.enter_context(tc.tile_pool(name="stream", bufs=3))
         planes_psum = ctx.enter_context(tc.psum_pool(name="planes_psum", bufs=4))
         sums_psum = ctx.enter_context(tc.psum_pool(name="sums_psum", bufs=4))
+        ctx.enter_context(tc.manual_schedule())
 
         identity = keep.tile([P, P], F32)
         masks.make_identity(nc, identity[:])

from contextlib import ExitStack

import concourse.masks as masks
import concourse.mybir as mybir

F32 = mybir.dt.float32
BF16 = mybir.dt.bfloat16
U32 = mybir.dt.uint32
U8 = mybir.dt.uint8
FP8X4 = mybir.dt.float8_e4m3fn_x4
MULT = mybir.AluOpType.mult
ADD = mybir.AluOpType.add

P = 128
K = 512
PACK = 4
PLANES_PER_BANK = 4
HEADS = 16
UNIT = 64
HALF = UNIT // 2
UNITS_PER_HEAD = 3
Q_COLS = HEADS * UNITS_PER_HEAD * UNIT
CHUNK = 512
CHUNK_ROWS = [CHUNK] * (Q_COLS // CHUNK)
CHUNKS = len(CHUNK_ROWS)
CHUNK_START = [sum(CHUNK_ROWS[:c]) for c in range(CHUNKS)]
LEAD = 2
LAG = 1

FLOPS = 2 * P * K * (K + Q_COLS + P)


def transpose_planes(nc, planes_psum, raw, first_plane, planes, identity):
    words = raw[:].bitcast(F32)
    bank = planes_psum.tile([P, planes, P], F32, tag="planes")
    for i in range(planes):
        plane = first_plane + i
        nc.tensor.transpose(bank[:, i, :], words[:, plane * P : (plane + 1) * P], identity[:])
    return bank


def rotary_products(nc, stream, rotary, cos_sb, sin_sb, result, heads):
    cos_all = cos_sb[:].unsqueeze(1).to_broadcast([P, heads, UNIT])
    sin_low = sin_sb[:, 0:HALF].unsqueeze(1).to_broadcast([P, heads, HALF])
    sin_high = sin_sb[:, HALF:UNIT].unsqueeze(1).to_broadcast([P, heads, HALF])
    crossed = stream.tile([P, UNITS_PER_HEAD, UNIT], F32, tag="crossed")
    nc.vector.tensor_tensor(out=result, in0=rotary, in1=cos_all, op=MULT)
    nc.vector.tensor_tensor(
        out=crossed[:, 0:heads, 0:HALF], in0=rotary[:, :, HALF:UNIT], in1=sin_low, op=MULT
    )
    nc.vector.tensor_tensor(
        out=crossed[:, 0:heads, HALF:UNIT], in0=rotary[:, :, 0:HALF], in1=sin_high, op=MULT
    )
    return crossed[:, 0:heads, :]


def tile_mlaselfattn_s_kernel(tc, x, cos, sin, Wqa, Wqb, Wkva, out):
    nc = tc.nc
    out_rows = out.flatten_outer_dims()

    with ExitStack() as ctx:
        keep = ctx.enter_context(tc.tile_pool(name="keep", bufs=1))
        stream = ctx.enter_context(tc.tile_pool(name="stream", bufs=3))
        planes_psum = ctx.enter_context(tc.psum_pool(name="planes_psum", bufs=4))
        sums_psum = ctx.enter_context(tc.psum_pool(name="sums_psum", bufs=4))
        ctx.enter_context(tc.manual_schedule())

        identity = keep.tile([P, P], F32)
        masks.make_identity(nc, identity[:])

        x_raw = keep.tile([P, K], BF16)
        nc.sync.dma_start(out=x_raw[:], in_=x.flatten_outer_dims())
        wqa_raw = []
        for u in range(2):
            raw = keep.tile([P, 2 * K], BF16, name="wqa_raw%d" % u)
            nc.sync.dma_start(
                out=raw[:],
                in_=Wqa[u * 2 * P : (u + 1) * 2 * P, :].rearrange("(p e) h -> p (e h)", e=2),
            )
            wqa_raw.append(raw)
        kva_raw = keep.tile([P, K], BF16)
        nc.sync.dma_start(out=kva_raw[:], in_=Wkva)
        wqb_raw = []
        for c in range(CHUNKS):
            raw = keep.tile([P, CHUNK_ROWS[c] // P * K], BF16, name="wqb_raw%d" % c)
            nc.sync.dma_start(
                out=raw[:],
                in_=Wqb[CHUNK_START[c] : CHUNK_START[c] + CHUNK_ROWS[c], :].rearrange(
                    "(p j) k -> p (j k)", p=P
                ),
            )
            wqb_raw.append(raw)
        cos_sb = keep.tile([P, UNIT], BF16)
        sin_sb = keep.tile([P, UNIT], BF16)
        nc.scalar.dma_start(out=cos_sb[:], in_=cos.flatten_outer_dims())
        nc.scalar.dma_start(out=sin_sb[:], in_=sin.flatten_outer_dims())

        x_codes = keep.tile([P, P], U32, align_bytes=64)
        x_scales = keep.tile([P, P], U8, align_bytes=64)
        kva_codes = keep.tile([P, P], U32, align_bytes=64)
        kva_scales = keep.tile([P, P], U8, align_bytes=64)
        wqa_codes = keep.tile([P, K], U32, align_bytes=64)
        wqa_scales = keep.tile([P, K], U8, align_bytes=64)
        qa_codes = keep.tile([P, P], U32, align_bytes=64)
        qa_scales = keep.tile([P, P], U8, align_bytes=64)
        wqb_codes = keep.tile([P, Q_COLS], U32, align_bytes=64)
        wqb_scales = keep.tile([P, Q_COLS], U8, align_bytes=64)
        out_sb = keep.tile([P, Q_COLS + 2 * UNIT], F32)

        def prepare_blocks(raw, slots, codes, scales):
            bank = transpose_planes(nc, planes_psum, raw, 0, 2 * slots, identity)
            grouped = stream.tile([P, slots * P * PACK], BF16, tag="grouped_blocks", align_bytes=64)
            nc.scalar.copy(
                out=grouped[:].bitcast(F32).rearrange("k (r c u) -> k r c u", r=slots, u=2),
                in_=bank[:].rearrange("k (r u) c -> k r c u", u=2),
            )
            nc.vector.quantize_mx(out=codes.bitcast(FP8X4), scales=scales, in_=grouped[:])

        grouped_chunks = {}

        def transpose_chunk(c):
            planes = 2 * CHUNK_ROWS[c] // P
            grouped = stream.tile(
                [P, CHUNK_ROWS[c] * PACK], BF16, tag="grouped_chunk", name="grouped%d" % c,
                align_bytes=64,
            )
            grouped_words = grouped[:].bitcast(F32).rearrange("k (c m) -> k c m", m=planes)
            for first in range(0, planes, PLANES_PER_BANK):
                count = min(PLANES_PER_BANK, planes - first)
                bank = transpose_planes(nc, planes_psum, wqb_raw[c], first, count, identity)
                nc.scalar.copy(
                    out=grouped_words[:, :, first : first + count],
                    in_=bank[:].rearrange("k m c -> k c m"),
                )
            grouped_chunks[c] = grouped

        def chunk_cols(c):
            return slice(CHUNK_START[c], CHUNK_START[c] + CHUNK_ROWS[c])

        def quantise_chunk(c):
            nc.vector.quantize_mx(
                out=wqb_codes[:, chunk_cols(c)].bitcast(FP8X4),
                scales=wqb_scales[:, chunk_cols(c)],
                in_=grouped_chunks[c][:],
            )

        def multiply_chunk(c):
            q_ps = sums_psum.tile([P, CHUNK_ROWS[c]], F32, tag="sums")
            nc.tensor.matmul_mx(
                out=q_ps[:],
                lhsT=qa_codes[:].bitcast(FP8X4),
                lhsT_scale=qa_scales[:],
                rhs=wqb_codes[:, chunk_cols(c)].bitcast(FP8X4),
                rhs_scale=wqb_scales[:, chunk_cols(c)],
                start=True,
                stop=True,
            )
            return q_ps

        def chunk_parts(c, q_ps):
            q_units = q_ps[:].rearrange("p (g w) -> p g w", w=UNIT)
            out_units = out_sb[:, chunk_cols(c)].rearrange("p (g w) -> p g w", w=UNIT)
            first = [(part - CHUNK_START[c] // UNIT) % UNITS_PER_HEAD for part in range(UNITS_PER_HEAD)]
            return [
                (q_units[:, f::UNITS_PER_HEAD, :], out_units[:, f::UNITS_PER_HEAD, :]) for f in first
            ]

        def multiply_rotary(rotary, rotated):
            crossed = rotary_products(nc, stream, rotary, cos_sb, sin_sb, rotated, rotary.shape[1])
            return rotated, crossed

        def add_rotary(products):
            rotated, crossed = products
            nc.vector.tensor_tensor(out=rotated, in0=rotated, in1=crossed, op=ADD)

        prepare_blocks(x_raw, 1, x_codes[:], x_scales[:])
        for u in range(2):
            cols = slice(u * 2 * P, (u + 1) * 2 * P)
            prepare_blocks(wqa_raw[u], 2, wqa_codes[:, cols], wqa_scales[:, cols])
        prepare_blocks(kva_raw, 1, kva_codes[:], kva_scales[:])
        transpose_chunk(0)

        qaT_ps = sums_psum.tile([P, PACK, P], F32, tag="sums")
        for t in range(PACK):
            nc.tensor.matmul_mx(
                out=qaT_ps[:, t, :],
                lhsT=wqa_codes[:, t * P : (t + 1) * P].bitcast(FP8X4),
                lhsT_scale=wqa_scales[:, t * P : (t + 1) * P],
                rhs=x_codes[:].bitcast(FP8X4),
                rhs_scale=x_scales[:],
                start=True,
                stop=True,
            )
        kv_ps = sums_psum.tile([P, 2, UNIT], F32, tag="sums")
        nc.tensor.matmul_mx(
            out=kv_ps[:].rearrange("p g w -> p (g w)"),
            lhsT=x_codes[:].bitcast(FP8X4),
            lhsT_scale=x_scales[:],
            rhs=kva_codes[:].bitcast(FP8X4),
            rhs_scale=kva_scales[:],
            start=True,
            stop=True,
        )
        qa_grouped = keep.tile([P, P, PACK], BF16, align_bytes=64)
        nc.vector.tensor_copy(out=qa_grouped[:], in_=qaT_ps[:].rearrange("k t n -> k n t"))
        quantise_chunk(0)
        nc.vector.quantize_mx(
            out=qa_codes[:].bitcast(FP8X4),
            scales=qa_scales[:],
            in_=qa_grouped[:].rearrange("k n t -> k (n t)"),
        )
        transpose_chunk(1)
        tail_units = out_sb[:, Q_COLS : Q_COLS + 2 * UNIT].rearrange("p (g w) -> p g w", w=UNIT)
        nc.scalar.copy(out=tail_units[:, 1:2, :], in_=kv_ps[:, 0:1, :])
        nc.vector.tensor_scalar_mul(out=sin_sb[:, 0:HALF], in0=sin_sb[:, 0:HALF], scalar1=-1.0)
        products = {-LAG: multiply_rotary(kv_ps[:, 1:2, :], tail_units[:, 0:1, :])}

        parts = {}
        for step in range(CHUNKS + LAG):
            ahead = step + LEAD
            done = step - LAG
            if ahead < CHUNKS:
                transpose_chunk(ahead)
            if step < CHUNKS:
                parts[step] = chunk_parts(step, multiply_chunk(step))
            if step + 1 < CHUNKS:
                quantise_chunk(step + 1)
            add_rotary(products[done])
            if step < CHUNKS:
                products[step] = multiply_rotary(parts[step][2][0], parts[step][2][1])
            if done >= 0:
                for part in range(UNITS_PER_HEAD - 1):
                    nc.scalar.copy(out=parts[done][part][1], in_=parts[done][part][0])
                first_col = CHUNK_START[done]
                last_col = CHUNK_START[done + 1] if done + 1 < CHUNKS else Q_COLS + 2 * UNIT
                nc.sync.dma_start(
                    out=out_rows[:, first_col:last_col], in_=out_sb[:, first_col:last_col]
                )
